import numpy as np
import ml_dtypes


def mxq(x, axis, fmt="e4m3"):
    dtype, down = {"e4m3": (ml_dtypes.float8_e4m3fn, 7), "e5m2": (ml_dtypes.float8_e5m2, 14)}[fmt]
    v = np.moveaxis(np.asarray(x, np.float32).astype(ml_dtypes.bfloat16).astype(np.float64), axis, -1)
    blocks = v.reshape(v.shape[:-1] + (-1, 32))
    amax = np.abs(blocks).max(-1, keepdims=True)
    byte = np.maximum(np.where(amax > 0, np.frexp(amax)[1] - 1 + 127, 0) - down, 1)
    scale = np.exp2(byte - 127.0)
    codes = (blocks / scale).astype(np.float32).astype(dtype).astype(np.float64)
    return np.moveaxis((codes * scale).reshape(v.shape), -1, axis)


WIDE = False


def mx_kscale(k):
    if not WIDE:
        return np.ones(k)
    levels = np.array([10, -10, 5, -5, 0])
    a = np.random.permutation(np.resize(levels, k // 512 * 4)).reshape(k // 512, 4)
    idx = np.arange(k)
    return np.exp2(a[idx // 512, idx % 128 // 32])


BF16 = ml_dtypes.bfloat16


def bf(x):
    return np.asarray(x, np.float32).astype(BF16)


def f64(x):
    return np.asarray(x).astype(np.float64)


B, S, DIM, H, C, NOPE, ROPE, VDIM = 2, 512, 2048, 8, 512, 64, 128, 128
THETA = 10000.0
EPS = 1e-6


def rope_tables():
    freqs = 1.0 / THETA ** (np.arange(0, ROPE, 2, dtype=np.float64) / ROPE)
    ang = np.outer(np.arange(S, dtype=np.float64), freqs)
    return np.cos(ang), np.sin(ang)


def setup_inputs():
    s = mx_kscale(DIM)
    return {"x": bf(np.random.standard_normal((B, S, DIM)) * s),
            "wkv_a": bf(np.random.standard_normal((C + ROPE, DIM)) / np.sqrt(DIM) / s),
            "kv_norm_w": bf(1.0 + 0.1 * np.random.standard_normal(C))}


def reference(x, wkv_a, kv_norm_w):
    kv = mxq(f64(x), 2, "e4m3") @ mxq(f64(wkv_a), 1, "e4m3").T
    kv_lat, k_raw = kv[..., :C], kv[..., C:]
    cos, sin = rope_tables()
    x0, x1 = k_raw[..., 0::2], k_raw[..., 1::2]
    r0 = x0 * cos - x1 * sin
    r1 = x0 * sin + x1 * cos
    k_pe = np.stack([r0, r1], axis=-1).reshape(B, S, ROPE)
    rms = np.sqrt(np.mean(kv_lat * kv_lat, axis=-1, keepdims=True) + EPS)
    kv_cache = kv_lat / rms * f64(kv_norm_w)
    return kv_cache, k_pe

@@ -1,0 +1,282 @@
+import math
+
+import concourse.mybir as mybir
+from concourse.masks import make_identity
+
+F32 = mybir.dt.float32
+BF16 = mybir.dt.bfloat16
+I32 = mybir.dt.int32
+U32 = mybir.dt.uint32
+U8 = mybir.dt.uint8
+FP8X4 = mybir.dt.float8_e4m3fn_x4
+ALU = mybir.AluOpType
+ACT = mybir.ActivationFunctionType
+
+P = 128
+BATCH = 2
+SEQ = 512
+DIM = 2048
+LATENT = 512
+ROPE = 128
+PAIRS = ROPE // 2
+DOUBLINGS = 6
+assert 2**DOUBLINGS == PAIRS
+THETA = 10000.0
+EPS = 1e-6
+
+K_PASS = 4 * P
+PASSES = DIM // K_PASS
+WORDS = DIM // 2
+BLOCKS_PER_BANK = 4
+BANKS_PER_TILE = WORDS // P // BLOCKS_PER_BANK
+X_TILES = BATCH * SEQ // P
+SEQ_TILES = SEQ // P
+W_TILES = (LATENT + ROPE) // P
+
+TWO_PI = 2.0 * math.pi
+ROUND_MAGIC = 1.5 * 2.0**23
+
+FLOPS = 2 * BATCH * SEQ * DIM * (LATENT + ROPE)
+
+
+def tile_simplemla_pa_kernel(tc, x, wkv_a, kv_norm_w, out_0, out_1):
+    nc = tc.nc
+    x_rows = x.flatten_outer_dims()
+    kv_cache_rows = out_0.flatten_outer_dims()
+
+    with (
+        tc.tile_pool(name="const", bufs=1) as const,
+        tc.tile_pool(name="raw", bufs=1) as raw,
+        tc.tile_pool(name="stage", bufs=3) as stage,
+        tc.tile_pool(name="quant", bufs=1) as quant,
+        tc.tile_pool(name="work", bufs=3) as work,
+        tc.psum_pool(name="psum_t", bufs=3) as psum_t,
+        tc.psum_pool(name="psum_lat", bufs=3) as psum_lat,
+        tc.psum_pool(name="psum_rope", bufs=2) as psum_rope,
+        tc.manual_schedule(),
+    ):
+        gain_rows = const.tile([P, LATENT], BF16)
+        nc.vector.memset(gain_rows[:], 0.0)
+        nc.scalar.dma_start(out=gain_rows[0:1, :], in_=kv_norm_w.rearrange("(o c) -> o c", o=1))
+        w_raw = []
+        for n in range(W_TILES):
+            w_tile = raw.tile([P, DIM], BF16, name="w_raw%d" % n)
+            nc.sync.dma_start(out=w_tile[:], in_=wkv_a[n * P : (n + 1) * P, :])
+            w_raw.append(w_tile)
+        x_raw = []
+        for m in range(X_TILES):
+            x_tile = raw.tile([P, DIM], BF16, name="x_raw%d" % m)
+            nc.sync.dma_start(out=x_tile[:], in_=x_rows[m * P : (m + 1) * P, :])
+            x_raw.append(x_tile)
+
+        position_int = const.tile([P, SEQ_TILES], I32)
+        nc.gpsimd.iota(position_int[:], pattern=[[P, SEQ_TILES]], base=0, channel_multiplier=1)
+        identity = const.tile([P, P], F32)
+        make_identity(nc, identity[:])
+        ones = const.tile([P, P], BF16)
+        nc.vector.memset(ones[:], 1.0)
+        eps = const.tile([P, 1], F32)
+        nc.vector.memset(eps[:], EPS)
+
+        position = const.tile([P, SEQ_TILES], F32)
+        nc.vector.tensor_copy(out=position[:], in_=position_int[:])
+        frequency = const.tile([P, PAIRS], F32)
+        nc.vector.memset(frequency[:, 0:1], 1.0)
+        for doubling in range(DOUBLINGS):
+            n = 2**doubling
+            nc.vector.tensor_scalar(
+                out=frequency[:, n : 2 * n],
+                in0=frequency[:, 0:n],
+                scalar1=THETA ** (-n / PAIRS),
+                scalar2=None,
+                op0=ALU.mult,
+            )
+        table_shape = [P, SEQ_TILES, PAIRS]
+        turns = const.tile([P, 2, SEQ_TILES, PAIRS], F32)
+        nc.vector.scalar_tensor_tensor(
+            out=turns[:, 0],
+            in0=frequency[:].unsqueeze(1).to_broadcast(table_shape),
+            scalar=1.0 / TWO_PI,
+            in1=position[:].unsqueeze(2).to_broadcast(table_shape),
+            op0=ALU.mult,
+            op1=ALU.mult,
+        )
+        nc.vector.tensor_scalar(
+            out=turns[:, 1], in0=turns[:, 0], scalar1=0.25, scalar2=None, op0=ALU.add
+        )
+        whole_turns = const.tile([P, 2, SEQ_TILES, PAIRS], F32)
+        nc.vector.tensor_scalar(
+            out=whole_turns[:],
+            in0=turns[:],
+            scalar1=ROUND_MAGIC,
+            scalar2=ROUND_MAGIC,
+            op0=ALU.add,
+            op1=ALU.subtract,
+        )
+        part_turns = const.tile([P, 2, SEQ_TILES * PAIRS], F32)
+        nc.vector.tensor_tensor(
+            out=part_turns[:].rearrange("p s c -> p (s c)"),
+            in0=turns[:].rearrange("p s t j -> p (s t j)"),
+            in1=whole_turns[:].rearrange("p s t j -> p (s t j)"),
+            op=ALU.subtract,
+        )
+        sin_table = const.tile([P, SEQ_TILES, PAIRS], F32)
+        nc.scalar.activation(
+            out=sin_table[:].rearrange("p t j -> p (t j)"),
+            in_=part_turns[:, 0, :],
+            func=ACT.Sin,
+            scale=TWO_PI,
+        )
+        cos_pairs = const.tile([P, SEQ_TILES, PAIRS, 2], F32)
+        nc.scalar.activation(
+            out=cos_pairs[:].rearrange("p t j e -> p (t j) e"),
+            in_=part_turns[:, 1, :].unsqueeze(2).to_broadcast([P, SEQ_TILES * PAIRS, 2]),
+            func=ACT.Sin,
+            scale=TWO_PI,
+        )
+        table_warmer = const.tile([P, 1], F32)
+        nc.scalar.activation(out=table_warmer[:], in_=eps[:], func=ACT.Sqrt)
+
+        gain_bank = psum_t.tile([P, LATENT], F32, tag="bank")
+        nc.tensor.matmul(out=gain_bank[:], lhsT=ones[:], rhs=gain_rows[:], start=True, stop=True)
+        gain = const.tile([P, LATENT], F32)
+        nc.vector.tensor_copy(out=gain[:], in_=gain_bank[:])
+
+        def transpose_rows(rows, copies):
+            words = rows[:].bitcast(F32)
+            grouped = stage.tile([P, PASSES * P * 4], BF16, align_bytes=64)
+            grouped_words = grouped[:].bitcast(F32).rearrange(
+                "p (g r u) -> p g r u", g=PASSES, u=2
+            )
+            for h in range(BANKS_PER_TILE):
+                bank = psum_t.tile([P, 2, 2, P], F32, tag="bank")
+                for g in range(2):
+                    for u in range(2):
+                        b = BLOCKS_PER_BANK * h + 2 * g + u
+                        nc.tensor.transpose(
+                            bank[:, g, u, :], words[:, b * P : (b + 1) * P], identity[:]
+                        )
+                copies[h](
+                    out=grouped_words[:, 2 * h : 2 * h + 2],
+                    in_=bank[:].rearrange("p g u r -> p g r u"),
+                )
+            return grouped
+
+        w_codes = quant.tile([P, PASSES, LATENT + ROPE], U32, align_bytes=64)
+        w_scales = quant.tile([P, PASSES, LATENT + ROPE], U8, align_bytes=64)
+
+        def quantise_weights(n, grouped):
+            for g in range(PASSES):
+                nc.vector.quantize_mx(
+                    out=w_codes[:, g, n * P : (n + 1) * P].bitcast(FP8X4),
+                    scales=w_scales[:, g, n * P : (n + 1) * P],
+                    in_=grouped[:, g * 4 * P : (g + 1) * 4 * P],
+                )
+
+        x_codes = {}
+        x_scales = {}
+
+        def quantise_tokens(m, grouped):
+            x_codes[m] = quant.tile([P, PASSES * P], U32, align_bytes=64, name="x_codes", bufs=3)
+            x_scales[m] = quant.tile([P, PASSES * P], U8, align_bytes=64, name="x_scales", bufs=3)
+            nc.vector.quantize_mx(
+                out=x_codes[m][:].bitcast(FP8X4), scales=x_scales[m][:], in_=grouped[:]
+            )
+
+        def multiply(m, out, columns):
+            for g in range(PASSES):
+                nc.tensor.matmul_mx(
+                    out=out,
+                    lhsT=x_codes[m][:, g * P : (g + 1) * P].bitcast(FP8X4),
+                    lhsT_scale=x_scales[m][:, g * P : (g + 1) * P],
+                    rhs=w_codes[:, g, columns].bitcast(FP8X4),
+                    rhs_scale=w_scales[:, g, columns],
+                    start=(g == 0),
+                    stop=(g == PASSES - 1),
+                )
+
+        def root_mean_square(latent):
+            squares = work.tile([P, LATENT], BF16)
+            sum_squares = work.tile([P, 1], F32)
+            nc.scalar.activation(
+                out=squares[:], in_=latent[:], func=ACT.Square, accum_out=sum_squares[:]
+            )
+            rms = work.tile([P, 1], F32)
+            nc.scalar.activation(
+                out=rms[:], in_=sum_squares[:], func=ACT.Sqrt, scale=1.0 / LATENT, bias=eps[:, 0:1]
+            )
+            return rms
+
+        def normalise(m, latent, rms):
+            inverse_rms = work.tile([P, 1], F32)
+            nc.vector.reciprocal(out=inverse_rms[:], in_=rms[:])
+            kv_cache = work.tile([P, LATENT], F32, bufs=4)
+            nc.vector.scalar_tensor_tensor(
+                out=kv_cache[:],
+                in0=latent[:],
+                scalar=inverse_rms[:, 0:1],
+                in1=gain[:],
+                op0=ALU.mult,
+                op1=ALU.mult,
+            )
+            nc.sync.dma_start(out=kv_cache_rows[m * P : (m + 1) * P, :], in_=kv_cache[:])
+
+        def rotate(t, raw_key, k_pe):
+            pairs = raw_key[:].rearrange("p (j e) -> p j e", e=2)
+            with_cos = work.tile([P, PAIRS, 2], F32)
+            nc.vector.tensor_tensor(out=with_cos[:], in0=pairs, in1=cos_pairs[:, t], op=ALU.mult)
+            with_sin = work.tile([P, 2, PAIRS], F32)
+            nc.vector.scalar_tensor_tensor(
+                out=with_sin[:, 0, :],
+                in0=pairs[:, :, 1],
+                scalar=-1.0,
+                in1=sin_table[:, t],
+                op0=ALU.mult,
+                op1=ALU.mult,
+            )
+            nc.vector.tensor_tensor(
+                out=with_sin[:, 1, :], in0=pairs[:, :, 0], in1=sin_table[:, t], op=ALU.mult
+            )
+            nc.vector.tensor_tensor(
+                out=k_pe, in0=with_cos[:], in1=with_sin[:].rearrange("p e j -> p j e"), op=ALU.add
+            )
+
+        shared_copies = [nc.vector.tensor_copy, nc.scalar.copy]
+        scalar_copies = [nc.scalar.copy, nc.scalar.copy]
+        grouped_w = {}
+        for n in range(W_TILES):
+            grouped_w[n] = transpose_rows(w_raw[n], shared_copies)
+            if n > 0:
+                quantise_weights(n - 1, grouped_w[n - 1])
+
+        grouped_x = {0: transpose_rows(x_raw[0], scalar_copies)}
+        quantise_weights(W_TILES - 1, grouped_w[W_TILES - 1])
+        grouped_x[1] = transpose_rows(x_raw[1], scalar_copies)
+        quantise_tokens(0, grouped_x[0])
+        latent = {}
+        rms = {}
+        k_pe = None
+        for m in range(X_TILES + 1):
+            if m < X_TILES:
+                raw_key = psum_rope.tile([P, ROPE], F32)
+                multiply(m, raw_key[:], slice(LATENT, LATENT + ROPE))
+                latent[m] = psum_lat.tile([P, LATENT], F32, name="latent")
+                multiply(m, latent[m][:], slice(0, LATENT))
+            if m > 0:
+                rms[m - 1] = root_mean_square(latent[m - 1])
+            if m + 2 < X_TILES:
+                grouped_x[m + 2] = transpose_rows(x_raw[m + 2], scalar_copies)
+            if m + 1 < X_TILES:
+                quantise_tokens(m + 1, grouped_x[m + 1])
+            if m < X_TILES:
+                t = m % SEQ_TILES
+                if t == 0:
+                    k_pe = work.tile([P, SEQ_TILES, PAIRS, 2], F32, bufs=2)
+                rotate(t, raw_key, k_pe[:, t])
+                if t == SEQ_TILES - 1:
+                    nc.sync.dma_start(
+                        out=out_1[m // SEQ_TILES].rearrange("(t p) c -> p t c", p=P),
+                        in_=k_pe[:].rearrange("p t j e -> p t (j e)"),
+                    )
+            if m > 0:
+                normalise(m - 1, latent[m - 1], rms[m - 1])

@@ -43,6 +43,7 @@ def tile_simplemla_pa_kernel(tc, x, wkv_a, kv_norm_w, out_0, out_1):
     nc = tc.nc
     x_rows = x.flatten_outer_dims()
     kv_cache_rows = out_0.flatten_outer_dims()
+    k_pe_rows = out_1.flatten_outer_dims()
 
     with (
         tc.tile_pool(name="const", bufs=1) as const,
@@ -135,12 +136,7 @@ def tile_simplemla_pa_kernel(tc, x, wkv_a, kv_norm_w, out_0, out_1):
             scale=TWO_PI,
         )
         table_warmer = const.tile([P, 1], F32)
-        nc.scalar.activation(out=table_warmer[:], in_=eps[:], func=ACT.Sqrt)
-
-        gain_bank = psum_t.tile([P, LATENT], F32, tag="bank")
-        nc.tensor.matmul(out=gain_bank[:], lhsT=ones[:], rhs=gain_rows[:], start=True, stop=True)
-        gain = const.tile([P, LATENT], F32)
-        nc.vector.tensor_copy(out=gain[:], in_=gain_bank[:])
+        nc.scalar.activation(out=table_warmer[:], in_=eps[:], func=ACT.Abs_reciprocal_sqrt)
 
         def transpose_rows(rows, copies):
             words = rows[:].bitcast(F32)
@@ -195,21 +191,23 @@ def tile_simplemla_pa_kernel(tc, x, wkv_a, kv_norm_w, out_0, out_1):
                     stop=(g == PASSES - 1),
                 )
 
-        def root_mean_square(latent):
+        def inverse_root_mean_square(latent):
             squares = work.tile([P, LATENT], BF16)
             sum_squares = work.tile([P, 1], F32)
             nc.scalar.activation(
                 out=squares[:], in_=latent[:], func=ACT.Square, accum_out=sum_squares[:]
             )
-            rms = work.tile([P, 1], F32)
-            nc.scalar.activation(
-                out=rms[:], in_=sum_squares[:], func=ACT.Sqrt, scale=1.0 / LATENT, bias=eps[:, 0:1]
-            )
-            return rms
-
-        def normalise(m, latent, rms):
             inverse_rms = work.tile([P, 1], F32)
-            nc.vector.reciprocal(out=inverse_rms[:], in_=rms[:])
+            nc.scalar.activation(
+                out=inverse_rms[:],
+                in_=sum_squares[:],
+                func=ACT.Abs_reciprocal_sqrt,
+                scale=1.0 / LATENT,
+                bias=eps[:, 0:1],
+            )
+            return inverse_rms
+
+        def normalise(m, latent, inverse_rms):
             kv_cache = work.tile([P, LATENT], F32, bufs=4)
             nc.vector.scalar_tensor_tensor(
                 out=kv_cache[:],
@@ -221,24 +219,38 @@ def tile_simplemla_pa_kernel(tc, x, wkv_a, kv_norm_w, out_0, out_1):
             )
             nc.sync.dma_start(out=kv_cache_rows[m * P : (m + 1) * P, :], in_=kv_cache[:])
 
-        def rotate(t, raw_key, k_pe):
-            pairs = raw_key[:].rearrange("p (j e) -> p j e", e=2)
-            with_cos = work.tile([P, PAIRS, 2], F32)
-            nc.vector.tensor_tensor(out=with_cos[:], in0=pairs, in1=cos_pairs[:, t], op=ALU.mult)
-            with_sin = work.tile([P, 2, PAIRS], F32)
+        def rotation_products(t, raw_keys):
+            pairs = raw_keys[:].rearrange("p t (j e) -> p (t j) e", e=2)
+            sines = sin_table[:, t : t + 2].rearrange("p t j -> p (t j)")
+            with_cos = work.tile([P, 2 * PAIRS, 2], F32)
+            nc.vector.tensor_tensor(
+                out=with_cos[:],
+                in0=pairs,
+                in1=cos_pairs[:, t : t + 2].rearrange("p t j e -> p (t j) e"),
+                op=ALU.mult,
+            )
+            with_sin = work.tile([P, 2, 2 * PAIRS], F32)
             nc.vector.scalar_tensor_tensor(
                 out=with_sin[:, 0, :],
                 in0=pairs[:, :, 1],
                 scalar=-1.0,
-                in1=sin_table[:, t],
+                in1=sines,
                 op0=ALU.mult,
                 op1=ALU.mult,
             )
             nc.vector.tensor_tensor(
-                out=with_sin[:, 1, :], in0=pairs[:, :, 0], in1=sin_table[:, t], op=ALU.mult
+                out=with_sin[:, 1, :], in0=pairs[:, :, 0], in1=sines, op=ALU.mult
             )
+            return with_cos, with_sin
+
+        def rotation_sum(m, with_cos, with_sin):
+            k_pe = work.tile([P, 2 * PAIRS, 2], F32)
             nc.vector.tensor_tensor(
-                out=k_pe, in0=with_cos[:], in1=with_sin[:].rearrange("p e j -> p j e"), op=ALU.add
+                out=k_pe[:], in0=with_cos[:], in1=with_sin[:].rearrange("p e c -> p c e"), op=ALU.add
+            )
+            nc.sync.dma_start(
+                out=k_pe_rows[m * P : (m + 2) * P, :].rearrange("(t p) c -> p t c", p=P),
+                in_=k_pe[:].rearrange("p (t j) e -> p t (j e)", t=2),
             )
 
         shared_copies = [nc.vector.tensor_copy, nc.scalar.copy]
@@ -253,30 +265,32 @@ def tile_simplemla_pa_kernel(tc, x, wkv_a, kv_norm_w, out_0, out_1):
         quantise_weights(W_TILES - 1, grouped_w[W_TILES - 1])
         grouped_x[1] = transpose_rows(x_raw[1], scalar_copies)
         quantise_tokens(0, grouped_x[0])
+
+        gain_bank = psum_t.tile([P, LATENT], F32, tag="bank")
+        nc.tensor.matmul(out=gain_bank[:], lhsT=ones[:], rhs=gain_rows[:], start=True, stop=True)
+        gain = const.tile([P, LATENT], F32)
+        nc.vector.tensor_copy(out=gain[:], in_=gain_bank[:])
+
         latent = {}
-        rms = {}
-        k_pe = None
+        inverse_rms = {}
+        raw_keys = None
         for m in range(X_TILES + 1):
+            second_of_two = m < X_TILES and m % 2 == 1
             if m < X_TILES:
-                raw_key = psum_rope.tile([P, ROPE], F32)
-                multiply(m, raw_key[:], slice(LATENT, LATENT + ROPE))
+                if m % 2 == 0:
+                    raw_keys = psum_rope.tile([P, 2, ROPE], F32)
+                multiply(m, raw_keys[:, m % 2, :], slice(LATENT, LATENT + ROPE))
                 latent[m] = psum_lat.tile([P, LATENT], F32, name="latent")
                 multiply(m, latent[m][:], slice(0, LATENT))
             if m > 0:
-                rms[m - 1] = root_mean_square(latent[m - 1])
+                inverse_rms[m - 1] = inverse_root_mean_square(latent[m - 1])
             if m + 2 < X_TILES:
                 grouped_x[m + 2] = transpose_rows(x_raw[m + 2], scalar_copies)
             if m + 1 < X_TILES:
                 quantise_tokens(m + 1, grouped_x[m + 1])
-            if m < X_TILES:
-                t = m % SEQ_TILES
-                if t == 0:
-                    k_pe = work.tile([P, SEQ_TILES, PAIRS, 2], F32, bufs=2)
-                rotate(t, raw_key, k_pe[:, t])
-                if t == SEQ_TILES - 1:
-                    nc.sync.dma_start(
-                        out=out_1[m // SEQ_TILES].rearrange("(t p) c -> p t c", p=P),
-                        in_=k_pe[:].rearrange("p t j e -> p t (j e)"),
-                    )
+            if second_of_two:
+                with_cos, with_sin = rotation_products((m - 1) % SEQ_TILES, raw_keys)
             if m > 0:
-                normalise(m - 1, latent[m - 1], rms[m - 1])
+                normalise(m - 1, latent[m - 1], inverse_rms[m - 1])
+            if second_of_two:
+                rotation_sum(m - 1, with_cos, with_sin)

@@ -33,6 +33,9 @@ X_TILES = BATCH * SEQ // P
 SEQ_TILES = SEQ // P
 W_TILES = (LATENT + ROPE) // P
 
+FIRST_TOKEN_TILES = 2
+WARM_UP = 7
+
 TWO_PI = 2.0 * math.pi
 ROUND_MAGIC = 1.5 * 2.0**23
 
@@ -59,16 +62,20 @@ def tile_simplemla_pa_kernel(tc, x, wkv_a, kv_norm_w, out_0, out_1):
         gain_rows = const.tile([P, LATENT], BF16)
         nc.vector.memset(gain_rows[:], 0.0)
         nc.scalar.dma_start(out=gain_rows[0:1, :], in_=kv_norm_w.rearrange("(o c) -> o c", o=1))
-        w_raw = []
+
+        def load_rows(rows, name):
+            tile_of_rows = raw.tile([P, DIM], BF16, name=name)
+            nc.sync.dma_start(out=tile_of_rows[:], in_=rows)
+            return tile_of_rows
+
+        x_raw = {}
+        for m in range(FIRST_TOKEN_TILES):
+            x_raw[m] = load_rows(x_rows[m * P : (m + 1) * P, :], "x_raw%d" % m)
+        w_raw = {}
         for n in range(W_TILES):
-            w_tile = raw.tile([P, DIM], BF16, name="w_raw%d" % n)
-            nc.sync.dma_start(out=w_tile[:], in_=wkv_a[n * P : (n + 1) * P, :])
-            w_raw.append(w_tile)
-        x_raw = []
-        for m in range(X_TILES):
-            x_tile = raw.tile([P, DIM], BF16, name="x_raw%d" % m)
-            nc.sync.dma_start(out=x_tile[:], in_=x_rows[m * P : (m + 1) * P, :])
-            x_raw.append(x_tile)
+            w_raw[n] = load_rows(wkv_a[n * P : (n + 1) * P, :], "w_raw%d" % n)
+        for m in range(FIRST_TOKEN_TILES, X_TILES):
+            x_raw[m] = load_rows(x_rows[m * P : (m + 1) * P, :], "x_raw%d" % m)
 
         position_int = const.tile([P, SEQ_TILES], I32)
         nc.gpsimd.iota(position_int[:], pattern=[[P, SEQ_TILES]], base=0, channel_multiplier=1)
@@ -78,6 +85,16 @@ def tile_simplemla_pa_kernel(tc, x, wkv_a, kv_norm_w, out_0, out_1):
         nc.vector.memset(ones[:], 1.0)
         eps = const.tile([P, 1], F32)
         nc.vector.memset(eps[:], EPS)
+
+        zeros = const.tile([P, LATENT], BF16)
+        nc.vector.memset(zeros[:], 0.0)
+        idle_bank = psum_lat.tile([P, LATENT], F32, name="latent")
+
+        def keep_clock_up():
+            nc.tensor.matmul(out=idle_bank[:], lhsT=ones[:], rhs=zeros[:], start=True, stop=True)
+
+        for warm in range(WARM_UP):
+            keep_clock_up()
 
         position = const.tile([P, SEQ_TILES], F32)
         nc.vector.tensor_copy(out=position[:], in_=position_int[:])
@@ -255,16 +272,23 @@ def tile_simplemla_pa_kernel(tc, x, wkv_a, kv_norm_w, out_0, out_1):
 
         shared_copies = [nc.vector.tensor_copy, nc.scalar.copy]
         scalar_copies = [nc.scalar.copy, nc.scalar.copy]
-        grouped_w = {}
-        for n in range(W_TILES):
-            grouped_w[n] = transpose_rows(w_raw[n], shared_copies)
-            if n > 0:
-                quantise_weights(n - 1, grouped_w[n - 1])
 
-        grouped_x = {0: transpose_rows(x_raw[0], scalar_copies)}
-        quantise_weights(W_TILES - 1, grouped_w[W_TILES - 1])
-        grouped_x[1] = transpose_rows(x_raw[1], scalar_copies)
+        def transpose_early(rows):
+            grouped = transpose_rows(rows, shared_copies)
+            keep_clock_up()
+            return grouped
+
+        grouped_x = {}
+        grouped_x[0] = transpose_early(x_raw[0])
+        grouped_x[1] = transpose_early(x_raw[1])
         quantise_tokens(0, grouped_x[0])
+        grouped_w = {}
+        grouped_w[0] = transpose_early(w_raw[0])
+        quantise_tokens(1, grouped_x[1])
+        for n in range(1, W_TILES):
+            grouped_w[n] = transpose_early(w_raw[n])
+            quantise_weights(n - 1, grouped_w[n - 1])
+        quantise_weights(W_TILES - 1, grouped_w[W_TILES - 1])
 
         gain_bank = psum_t.tile([P, LATENT], F32, tag="bank")
         nc.tensor.matmul(out=gain_bank[:], lhsT=ones[:], rhs=gain_rows[:], start=True, stop=True)
@@ -275,22 +299,21 @@ def tile_simplemla_pa_kernel(tc, x, wkv_a, kv_norm_w, out_0, out_1):
         inverse_rms = {}
         raw_keys = None
         for m in range(X_TILES + 1):
-            second_of_two = m < X_TILES and m % 2 == 1
             if m < X_TILES:
+                latent[m] = psum_lat.tile([P, LATENT], F32, name="latent")
+                multiply(m, latent[m][:], slice(0, LATENT))
                 if m % 2 == 0:
                     raw_keys = psum_rope.tile([P, 2, ROPE], F32)
                 multiply(m, raw_keys[:, m % 2, :], slice(LATENT, LATENT + ROPE))
-                latent[m] = psum_lat.tile([P, LATENT], F32, name="latent")
-                multiply(m, latent[m][:], slice(0, LATENT))
             if m > 0:
                 inverse_rms[m - 1] = inverse_root_mean_square(latent[m - 1])
             if m + 2 < X_TILES:
                 grouped_x[m + 2] = transpose_rows(x_raw[m + 2], scalar_copies)
-            if m + 1 < X_TILES:
+            if FIRST_TOKEN_TILES <= m + 1 < X_TILES:
                 quantise_tokens(m + 1, grouped_x[m + 1])
-            if second_of_two:
-                with_cos, with_sin = rotation_products((m - 1) % SEQ_TILES, raw_keys)
             if m > 0:
                 normalise(m - 1, latent[m - 1], inverse_rms[m - 1])
-            if second_of_two:
-                rotation_sum(m - 1, with_cos, with_sin)
+            if m % 2 == 1:
+                with_cos, with_sin = rotation_products((m - 1) % SEQ_TILES, raw_keys)
+            if m % 2 == 0 and m > 0:
+                rotation_sum(m - 2, with_cos, with_sin)

import math

import concourse.mybir as mybir
from concourse.masks import make_identity

F32 = mybir.dt.float32
BF16 = mybir.dt.bfloat16
I32 = mybir.dt.int32
U32 = mybir.dt.uint32
U8 = mybir.dt.uint8
FP8X4 = mybir.dt.float8_e4m3fn_x4
ALU = mybir.AluOpType
ACT = mybir.ActivationFunctionType

P = 128
BATCH = 2
SEQ = 512
DIM = 2048
LATENT = 512
ROPE = 128
PAIRS = ROPE // 2
DOUBLINGS = 6
assert 2**DOUBLINGS == PAIRS
THETA = 10000.0
EPS = 1e-6

K_PASS = 4 * P
PASSES = DIM // K_PASS
WORDS = DIM // 2
BLOCKS_PER_BANK = 4
BANKS_PER_TILE = WORDS // P // BLOCKS_PER_BANK
X_TILES = BATCH * SEQ // P
SEQ_TILES = SEQ // P
W_TILES = (LATENT + ROPE) // P

FIRST_TOKEN_TILES = 2
WARM_UP = 7

TWO_PI = 2.0 * math.pi
ROUND_MAGIC = 1.5 * 2.0**23

FLOPS = 2 * BATCH * SEQ * DIM * (LATENT + ROPE)


def tile_simplemla_pa_kernel(tc, x, wkv_a, kv_norm_w, out_0, out_1):
    nc = tc.nc
    x_rows = x.flatten_outer_dims()
    kv_cache_rows = out_0.flatten_outer_dims()
    k_pe_rows = out_1.flatten_outer_dims()

    with (
        tc.tile_pool(name="const", bufs=1) as const,
        tc.tile_pool(name="raw", bufs=1) as raw,
        tc.tile_pool(name="stage", bufs=3) as stage,
        tc.tile_pool(name="quant", bufs=1) as quant,
        tc.tile_pool(name="work", bufs=3) as work,
        tc.psum_pool(name="psum_t", bufs=3) as psum_t,
        tc.psum_pool(name="psum_lat", bufs=3) as psum_lat,
        tc.psum_pool(name="psum_rope", bufs=2) as psum_rope,
        tc.manual_schedule(),
    ):
        gain_rows = const.tile([P, LATENT], BF16)
        nc.vector.memset(gain_rows[:], 0.0)
        nc.scalar.dma_start(out=gain_rows[0:1, :], in_=kv_norm_w.rearrange("(o c) -> o c", o=1))

        def load_rows(rows, name):
            tile_of_rows = raw.tile([P, DIM], BF16, name=name)
            nc.sync.dma_start(out=tile_of_rows[:], in_=rows)
            return tile_of_rows

        x_raw = {}
        for m in range(FIRST_TOKEN_TILES):
            x_raw[m] = load_rows(x_rows[m * P : (m + 1) * P, :], "x_raw%d" % m)
        w_raw = {}
        for n in range(W_TILES):
            w_raw[n] = load_rows(wkv_a[n * P : (n + 1) * P, :], "w_raw%d" % n)
        for m in range(FIRST_TOKEN_TILES, X_TILES):
            x_raw[m] = load_rows(x_rows[m * P : (m + 1) * P, :], "x_raw%d" % m)

        position_int = const.tile([P, SEQ_TILES], I32)
        nc.gpsimd.iota(position_int[:], pattern=[[P, SEQ_TILES]], base=0, channel_multiplier=1)
        identity = const.tile([P, P], F32)
        make_identity(nc, identity[:])
        ones = const.tile([P, P], BF16)
        nc.vector.memset(ones[:], 1.0)
        eps = const.tile([P, 1], F32)
        nc.vector.memset(eps[:], EPS)

        zeros = const.tile([P, LATENT], BF16)
        nc.vector.memset(zeros[:], 0.0)
        idle_bank = psum_lat.tile([P, LATENT], F32, name="latent")

        def keep_clock_up():
            nc.tensor.matmul(out=idle_bank[:], lhsT=ones[:], rhs=zeros[:], start=True, stop=True)

        for warm in range(WARM_UP):
            keep_clock_up()

        position = const.tile([P, SEQ_TILES], F32)
        nc.vector.tensor_copy(out=position[:], in_=position_int[:])
        frequency = const.tile([P, PAIRS], F32)
        nc.vector.memset(frequency[:, 0:1], 1.0)
        for doubling in range(DOUBLINGS):
            n = 2**doubling
            nc.vector.tensor_scalar(
                out=frequency[:, n : 2 * n],
                in0=frequency[:, 0:n],
                scalar1=THETA ** (-n / PAIRS),
                scalar2=None,
                op0=ALU.mult,
            )
        table_shape = [P, SEQ_TILES, PAIRS]
        turns = const.tile([P, 2, SEQ_TILES, PAIRS], F32)
        nc.vector.scalar_tensor_tensor(
            out=turns[:, 0],
            in0=frequency[:].unsqueeze(1).to_broadcast(table_shape),
            scalar=1.0 / TWO_PI,
            in1=position[:].unsqueeze(2).to_broadcast(table_shape),
            op0=ALU.mult,
            op1=ALU.mult,
        )
        nc.vector.tensor_scalar(
            out=turns[:, 1], in0=turns[:, 0], scalar1=0.25, scalar2=None, op0=ALU.add
        )
        whole_turns = const.tile([P, 2, SEQ_TILES, PAIRS], F32)
        nc.vector.tensor_scalar(
            out=whole_turns[:],
            in0=turns[:],
            scalar1=ROUND_MAGIC,
            scalar2=ROUND_MAGIC,
            op0=ALU.add,
            op1=ALU.subtract,
        )
        part_turns = const.tile([P, 2, SEQ_TILES * PAIRS], F32)
        nc.vector.tensor_tensor(
            out=part_turns[:].rearrange("p s c -> p (s c)"),
            in0=turns[:].rearrange("p s t j -> p (s t j)"),
            in1=whole_turns[:].rearrange("p s t j -> p (s t j)"),
            op=ALU.subtract,
        )
        sin_table = const.tile([P, SEQ_TILES, PAIRS], F32)
        nc.scalar.activation(
            out=sin_table[:].rearrange("p t j -> p (t j)"),
            in_=part_turns[:, 0, :],
            func=ACT.Sin,
            scale=TWO_PI,
        )
        cos_pairs = const.tile([P, SEQ_TILES, PAIRS, 2], F32)
        nc.scalar.activation(
            out=cos_pairs[:].rearrange("p t j e -> p (t j) e"),
            in_=part_turns[:, 1, :].unsqueeze(2).to_broadcast([P, SEQ_TILES * PAIRS, 2]),
            func=ACT.Sin,
            scale=TWO_PI,
        )
        table_warmer = const.tile([P, 1], F32)
        nc.scalar.activation(out=table_warmer[:], in_=eps[:], func=ACT.Abs_reciprocal_sqrt)

        def transpose_rows(rows, copies):
            words = rows[:].bitcast(F32)
            grouped = stage.tile([P, PASSES * P * 4], BF16, align_bytes=64)
            grouped_words = grouped[:].bitcast(F32).rearrange(
                "p (g r u) -> p g r u", g=PASSES, u=2
            )
            for h in range(BANKS_PER_TILE):
                bank = psum_t.tile([P, 2, 2, P], F32, tag="bank")
                for g in range(2):
                    for u in range(2):
                        b = BLOCKS_PER_BANK * h + 2 * g + u
                        nc.tensor.transpose(
                            bank[:, g, u, :], words[:, b * P : (b + 1) * P], identity[:]
                        )
                copies[h](
                    out=grouped_words[:, 2 * h : 2 * h + 2],
                    in_=bank[:].rearrange("p g u r -> p g r u"),
                )
            return grouped

        w_codes = quant.tile([P, PASSES, LATENT + ROPE], U32, align_bytes=64)
        w_scales = quant.tile([P, PASSES, LATENT + ROPE], U8, align_bytes=64)

        def quantise_weights(n, grouped):
            for g in range(PASSES):
                nc.vector.quantize_mx(
                    out=w_codes[:, g, n * P : (n + 1) * P].bitcast(FP8X4),
                    scales=w_scales[:, g, n * P : (n + 1) * P],
                    in_=grouped[:, g * 4 * P : (g + 1) * 4 * P],
                )

        x_codes = {}
        x_scales = {}

        def quantise_tokens(m, grouped):
            x_codes[m] = quant.tile([P, PASSES * P], U32, align_bytes=64, name="x_codes", bufs=3)
            x_scales[m] = quant.tile([P, PASSES * P], U8, align_bytes=64, name="x_scales", bufs=3)
            nc.vector.quantize_mx(
                out=x_codes[m][:].bitcast(FP8X4), scales=x_scales[m][:], in_=grouped[:]
            )

        def multiply(m, out, columns):
            for g in range(PASSES):
                nc.tensor.matmul_mx(
                    out=out,
                    lhsT=x_codes[m][:, g * P : (g + 1) * P].bitcast(FP8X4),
                    lhsT_scale=x_scales[m][:, g * P : (g + 1) * P],
                    rhs=w_codes[:, g, columns].bitcast(FP8X4),
                    rhs_scale=w_scales[:, g, columns],
                    start=(g == 0),
                    stop=(g == PASSES - 1),
                )

        def inverse_root_mean_square(latent):
            squares = work.tile([P, LATENT], BF16)
            sum_squares = work.tile([P, 1], F32)
            nc.scalar.activation(
                out=squares[:], in_=latent[:], func=ACT.Square, accum_out=sum_squares[:]
            )
            inverse_rms = work.tile([P, 1], F32)
            nc.scalar.activation(
                out=inverse_rms[:],
                in_=sum_squares[:],
                func=ACT.Abs_reciprocal_sqrt,
                scale=1.0 / LATENT,
                bias=eps[:, 0:1],
            )
            return inverse_rms

        def normalise(m, latent, inverse_rms):
            kv_cache = work.tile([P, LATENT], F32, bufs=4)
            nc.vector.scalar_tensor_tensor(
                out=kv_cache[:],
                in0=latent[:],
                scalar=inverse_rms[:, 0:1],
                in1=gain[:],
                op0=ALU.mult,
                op1=ALU.mult,
            )
            nc.sync.dma_start(out=kv_cache_rows[m * P : (m + 1) * P, :], in_=kv_cache[:])

        def rotation_products(t, raw_keys):
            pairs = raw_keys[:].rearrange("p t (j e) -> p (t j) e", e=2)
            sines = sin_table[:, t : t + 2].rearrange("p t j -> p (t j)")
            with_cos = work.tile([P, 2 * PAIRS, 2], F32)
            nc.vector.tensor_tensor(
                out=with_cos[:],
                in0=pairs,
                in1=cos_pairs[:, t : t + 2].rearrange("p t j e -> p (t j) e"),
                op=ALU.mult,
            )
            with_sin = work.tile([P, 2, 2 * PAIRS], F32)
            nc.vector.scalar_tensor_tensor(
                out=with_sin[:, 0, :],
                in0=pairs[:, :, 1],
                scalar=-1.0,
                in1=sines,
                op0=ALU.mult,
                op1=ALU.mult,
            )
            nc.vector.tensor_tensor(
                out=with_sin[:, 1, :], in0=pairs[:, :, 0], in1=sines, op=ALU.mult
            )
            return with_cos, with_sin

        def rotation_sum(m, with_cos, with_sin):
            k_pe = work.tile([P, 2 * PAIRS, 2], F32)
            nc.vector.tensor_tensor(
                out=k_pe[:], in0=with_cos[:], in1=with_sin[:].rearrange("p e c -> p c e"), op=ALU.add
            )
            nc.sync.dma_start(
                out=k_pe_rows[m * P : (m + 2) * P, :].rearrange("(t p) c -> p t c", p=P),
                in_=k_pe[:].rearrange("p (t j) e -> p t (j e)", t=2),
            )

        shared_copies = [nc.vector.tensor_copy, nc.scalar.copy]
        scalar_copies = [nc.scalar.copy, nc.scalar.copy]

        def transpose_early(rows):
            grouped = transpose_rows(rows, shared_copies)
            keep_clock_up()
            return grouped

        grouped_x = {}
        grouped_x[0] = transpose_early(x_raw[0])
        grouped_x[1] = transpose_early(x_raw[1])
        quantise_tokens(0, grouped_x[0])
        grouped_w = {}
        grouped_w[0] = transpose_early(w_raw[0])
        quantise_tokens(1, grouped_x[1])
        for n in range(1, W_TILES):
            grouped_w[n] = transpose_early(w_raw[n])
            quantise_weights(n - 1, grouped_w[n - 1])
        quantise_weights(W_TILES - 1, grouped_w[W_TILES - 1])

        gain_bank = psum_t.tile([P, LATENT], F32, tag="bank")
        nc.tensor.matmul(out=gain_bank[:], lhsT=ones[:], rhs=gain_rows[:], start=True, stop=True)
        gain = const.tile([P, LATENT], F32)
        nc.vector.tensor_copy(out=gain[:], in_=gain_bank[:])

        latent = {}
        inverse_rms = {}
        raw_keys = None
        for m in range(X_TILES + 1):
            if m < X_TILES:
                latent[m] = psum_lat.tile([P, LATENT], F32, name="latent")
                multiply(m, latent[m][:], slice(0, LATENT))
                if m % 2 == 0:
                    raw_keys = psum_rope.tile([P, 2, ROPE], F32)
                multiply(m, raw_keys[:, m % 2, :], slice(LATENT, LATENT + ROPE))
            if m > 0:
                inverse_rms[m - 1] = inverse_root_mean_square(latent[m - 1])
            if m + 2 < X_TILES:
                grouped_x[m + 2] = transpose_rows(x_raw[m + 2], scalar_copies)
            if FIRST_TOKEN_TILES <= m + 1 < X_TILES:
                quantise_tokens(m + 1, grouped_x[m + 1])
            if m > 0:
                normalise(m - 1, latent[m - 1], inverse_rms[m - 1])
            if m % 2 == 1:
                with_cos, with_sin = rotation_products((m - 1) % SEQ_TILES, raw_keys)
            if m % 2 == 0 and m > 0:
                rotation_sum(m - 2, with_cos, with_sin)
